import numpy as np
import ml_dtypes


def mxq(x, axis, fmt="e4m3"):
    dtype, down = {"e4m3": (ml_dtypes.float8_e4m3fn, 7), "e5m2": (ml_dtypes.float8_e5m2, 14)}[fmt]
    v = np.moveaxis(np.asarray(x, np.float32).astype(ml_dtypes.bfloat16).astype(np.float64), axis, -1)
    blocks = v.reshape(v.shape[:-1] + (-1, 32))
    amax = np.abs(blocks).max(-1, keepdims=True)
    byte = np.maximum(np.where(amax > 0, np.frexp(amax)[1] - 1 + 127, 0) - down, 1)
    scale = np.exp2(byte - 127.0)
    codes = (blocks / scale).astype(np.float32).astype(dtype).astype(np.float64)
    return np.moveaxis((codes * scale).reshape(v.shape), -1, axis)


WIDE = False


def mx_kscale(k):
    if not WIDE:
        return np.ones(k)
    levels = np.array([10, -10, 5, -5, 0])
    a = np.random.permutation(np.resize(levels, k // 512 * 4)).reshape(k // 512, 4)
    idx = np.arange(k)
    return np.exp2(a[idx // 512, idx % 128 // 32])


BF16 = ml_dtypes.bfloat16


def bf(x):
    return np.asarray(x, np.float32).astype(BF16)


def f64(x):
    return np.asarray(x).astype(np.float64)


B, T, N, DH, D = 1, 128, 4, 128, 512
KC = N * DH


def setup_inputs():
    r = np.random.standard_normal
    s = mx_kscale(D)
    t = mx_kscale(KC).reshape(N, DH)
    return {"normalized_resid_pre": bf(r((B, T, D)) * s),
            "W_C": bf(r((N, D, DH)) / np.sqrt(D) / s[None, :, None] * t[:, None, :]),
            "b_C": bf(0.1 * r((N, DH)) * t),
            "W_K": bf(1.3 / np.sqrt(KC) * r((N, DH, DH, DH)) / t[:, None, None, :])}


def reference(normalized_resid_pre, W_C, b_C, W_K):
    x = f64(normalized_resid_pre)
    wc = f64(W_C).transpose(1, 0, 2).reshape(D, KC)
    c = (mxq(x, 2, "e4m3") @ mxq(wc, 0, "e4m3")) + f64(b_C).reshape(KC)
    wk = f64(W_K).transpose(0, 3, 1, 2).reshape(KC, DH * DH)
    step1 = mxq(c, 2, "e4m3") @ mxq(wk, 0, "e4m3")
    return step1.reshape(B, T, DH, DH)

@@ -1,0 +1,254 @@
+from contextlib import ExitStack
+
+import concourse.mybir as mybir
+from concourse.masks import make_identity
+
+F32 = mybir.dt.float32
+BF16 = mybir.dt.bfloat16
+U32 = mybir.dt.uint32
+U8 = mybir.dt.uint8
+FP8X4 = mybir.dt.float8_e4m3fn_x4
+ADD = mybir.AluOpType.add
+
+P = 128
+T, D, N, DH = 128, 512, 4, 128
+IJ = DH * DH
+FLOPS = 2 * T * D * N * DH + 2 * T * N * DH * IJ
+
+ROWS = [8, 8, 16, 32, 32, 16, 8, 8]
+FIRST_LOADS = 5
+LAST_DONOR = 2
+MANUAL = True
+
+
+def tile_trittentioncube_pb_kernel(tc, normalized_resid_pre, W_C, b_C, W_K, out):
+    nc = tc.nc
+    assert sum(ROWS) * P == IJ
+    with ExitStack() as ctx:
+        const = ctx.enter_context(tc.tile_pool(name="const", bufs=1))
+        xpools = {
+            8: ctx.enter_context(tc.tile_pool(name="x8", bufs=8)),
+            16: ctx.enter_context(tc.tile_pool(name="x16", bufs=4)),
+            32: ctx.enter_context(tc.tile_pool(name="x32", bufs=8)),
+        }
+        opool = ctx.enter_context(tc.tile_pool(name="o", bufs=1))
+        gpool = ctx.enter_context(tc.tile_pool(name="g", bufs=3))
+        qpool = ctx.enter_context(tc.tile_pool(name="q", bufs=4))
+        pt = ctx.enter_context(tc.psum_pool(name="pt", bufs=4))
+        po = ctx.enter_context(tc.psum_pool(name="po", bufs=4))
+        if MANUAL:
+            ctx.enter_context(tc.manual_schedule())
+
+        wk = W_K.rearrange("n i j k -> n (i j) k")
+        out2 = out.rearrange("b t i j -> (b t) (i j)")
+
+        bases = [P * sum(ROWS[:g]) for g in range(len(ROWS))]
+        units = [(g, s) for g in range(len(ROWS)) for s in range(ROWS[g] // 4)]
+        n_units = len(units)
+        n_rounds = n_units // 2
+
+        ident = const.tile([P, P], F32, name="ident")
+        make_identity(nc, ident[:])
+        gc = const.tile([P, 4 * T * 4], BF16, name="gc", align_bytes=64)
+        nc.vector.memset(gc[:], 0.0)
+
+        x_sb = const.tile([P, D], BF16, name="x_sb")
+        nc.sync.dma_start(out=x_sb[:], in_=normalized_resid_pre.rearrange("b t d -> (b t) d"))
+        w_raw = const.tile([P, 8, 256], BF16, name="w_raw")
+        nc.sync.dma_start(
+            out=w_raw[:],
+            in_=W_C.rearrange("n d k -> (n d) k").rearrange("(g p e) k -> p g (e k)", g=8, p=P, e=2),
+        )
+        bv = b_C.rearrange("(a u) (w e) -> a w u e", a=2, u=2, w=64, e=2)
+        bias_bf = [const.tile([P, 4], BF16, name="bias_bf%d" % v) for v in range(2)]
+        for v in range(2):
+            for a in range(2):
+                half = a if v == 0 else 1 - a
+                nc.scalar.dma_start(
+                    out=bias_bf[v][half * 64 : (half + 1) * 64, :].rearrange("w (u e) -> w u e", u=2),
+                    in_=bv[a],
+                )
+
+        xt = {}
+
+        def load_chunk(g):
+            rows = ROWS[g]
+            for n in range(N):
+                t = xpools[rows].tile([P, rows * DH], BF16, name="x%d_%d_%d" % (rows, g, n), tag="x%d" % rows)
+                nc.sync.dma_start(
+                    out=t[:],
+                    in_=wk[n, bases[g] : bases[g] + P * rows, :].rearrange("(p r) k -> p (r k)", r=rows),
+                )
+                xt[(g, n)] = t
+
+        for g in range(FIRST_LOADS):
+            load_chunk(g)
+
+        tx = pt.tile([P, 512], F32, name="tx", tag="t")
+        xw = x_sb[:].bitcast(F32)
+        for u in range(2):
+            nc.tensor.transpose(tx[:, u * P : (u + 1) * P], xw[:, u * P : (u + 1) * P], ident[:])
+        gx = const.tile([P, 4 * T], BF16, name="gx", align_bytes=64)
+        nc.vector.tensor_copy(
+            out=gx[:].bitcast(F32).rearrange("q (c u) -> q c u", u=2),
+            in_=tx[:, 0 : 2 * P].rearrange("q (u c) -> q c u", u=2),
+        )
+        bias = [const.tile([P, 4], F32, name="bias%d" % v) for v in range(2)]
+        for v in range(2):
+            nc.vector.tensor_copy(out=bias[v][:], in_=bias_bf[v][:])
+        x_codes = const.tile([P, T], U32, name="x_codes", align_bytes=64)
+        x_scales = const.tile([P, T], U8, name="x_scales", align_bytes=64)
+        nc.vector.quantize_mx(out=x_codes[:].bitcast(FP8X4), scales=x_scales[:], in_=gx[:])
+
+        gw = const.tile([P, 4, 3, 64, 4], BF16, name="gw", align_bytes=64)
+        wv = w_raw[:].rearrange("p g f -> p (g f)").rearrange(
+            "p (a u t w e) -> p a u t w e", a=2, u=2, t=4, w=64, e=2
+        )
+        for u in range(2):
+            for e in range(2):
+                src = wv[:, :, u, :, :, e].rearrange("p a t w -> p a w t")
+                dst = gw[:, 2 * u + e, 0:2, :, :]
+                if u == 0:
+                    nc.vector.tensor_copy(out=dst, in_=src)
+                else:
+                    nc.scalar.copy(out=dst, in_=src)
+        nc.vector.tensor_copy(out=gw[:, :, 2, :, :], in_=gw[:, :, 0, :, :])
+        w_codes = const.tile([P, 768], U32, name="w_codes", align_bytes=64)
+        w_scales = const.tile([P, 768], U8, name="w_scales", align_bytes=64)
+        gwf = gw[:].rearrange("p s z w t -> p (s z w t)")
+        nc.vector.quantize_mx(out=w_codes[:, 0:512].bitcast(FP8X4), scales=w_scales[:, 0:512], in_=gwf[:, 0:2048])
+        nc.vector.quantize_mx(
+            out=w_codes[:, 512:768].bitcast(FP8X4), scales=w_scales[:, 512:768], in_=gwf[:, 2048:3072]
+        )
+        pc = []
+        for v in range(2):
+            acc = po.tile([P, 512], F32, name="pc%d" % v, tag="o")
+            for s in range(4):
+                lo = s * 192 + v * 64
+                nc.tensor.matmul_mx(
+                    out=acc[:, s * T : (s + 1) * T],
+                    lhsT=w_codes[:, lo : lo + P].bitcast(FP8X4),
+                    lhsT_scale=w_scales[:, lo : lo + P],
+                    rhs=x_codes[:].bitcast(FP8X4),
+                    rhs_scale=x_scales[:],
+                    start=True,
+                    stop=True,
+                )
+            pc.append(acc)
+        s_codes = const.tile([P, 4 * T], U32, name="s_codes", align_bytes=64)
+        s_scales = const.tile([P, 4 * T], U8, name="s_scales", align_bytes=64)
+
+        def finish_stage1():
+            for v in range(2):
+                for half in range(2):
+                    a = half if v == 0 else 1 - half
+                    slot = 2 * a + half
+                    rows = slice(half * 64, (half + 1) * 64)
+                    nc.vector.tensor_tensor(
+                        out=gc[rows, slot * 512 : (slot + 1) * 512].rearrange("m (c t) -> m c t", t=4),
+                        in0=pc[v][rows, :].rearrange("m (t c) -> m c t", t=4),
+                        in1=bias[v][rows, :].unsqueeze(1).to_broadcast([64, T, 4]),
+                        op=ADD,
+                    )
+            nc.vector.quantize_mx(out=s_codes[:].bitcast(FP8X4), scales=s_scales[:], in_=gc[:])
+
+        banks = {}
+        grouped = {}
+        quant = {}
+        obank = {}
+        otile = {}
+
+        def ok(j):
+            return 0 <= j < n_units
+
+        def transposes(j):
+            g, s = units[j]
+            for a in range(2):
+                bank = pt.tile([P, 512], F32, name="tb%d_%d" % (j, a), tag="t")
+                for u in range(2):
+                    xwv = xt[(g, 2 * a + u)][:].bitcast(F32)
+                    for l in range(2):
+                        off = (2 * s + l) * P
+                        col = (2 * u + l) * P
+                        nc.tensor.transpose(bank[:, col : col + P], xwv[:, off : off + P], ident[:])
+                banks[(j, a)] = bank
+
+        def regroup(j, a, eng):
+            if a == 0:
+                grouped[j] = gpool.tile([P, 2048], BF16, name="g%d" % j, tag="g", align_bytes=64)
+            dst = grouped[j][:].bitcast(F32)[:, a * 512 : (a + 1) * 512].rearrange("q (c u) -> q c u", u=2)
+            src = banks[(j, a)][:].rearrange("q (u c) -> q c u", u=2)
+            if eng == "s":
+                nc.scalar.copy(out=dst, in_=src)
+            else:
+                nc.vector.tensor_copy(out=dst, in_=src)
+
+        def quantise(j):
+            codes = qpool.tile([P, 512], U32, name="qc%d" % j, tag="qc", align_bytes=64)
+            scales = qpool.tile([P, 512], U8, name="qs%d" % j, tag="qs", align_bytes=64)
+            nc.vector.quantize_mx(out=codes[:].bitcast(FP8X4), scales=scales[:], in_=grouped[j][:])
+            quant[j] = (codes, scales)
+
+        def multiply(j):
+            codes, scales = quant[j]
+            acc = po.tile([P, 512], F32, name="ob%d" % j, tag="o")
+            for h in range(2):
+                for a in range(2):
+                    slot = 2 * a + h
+                    nc.tensor.matmul_mx(
+                        out=acc[:, h * 256 : (h + 1) * 256],
+                        lhsT=s_codes[:, slot * T : (slot + 1) * T].bitcast(FP8X4),
+                        lhsT_scale=s_scales[:, slot * T : (slot + 1) * T],
+                        rhs=codes[:, a * 256 : (a + 1) * 256].bitcast(FP8X4),
+                        rhs_scale=scales[:, a * 256 : (a + 1) * 256],
+                        start=(a == 0),
+                        stop=(a == 1),
+                    )
+            obank[j] = acc
+
+        finished = []
+        stored = [0]
+        late_loaded = [False]
+
+        def copy_out(j):
+            g, s = units[j]
+            rows = ROWS[g]
+            if s == 0:
+                otile[g] = opool.tile([P, P * rows], F32, name="o%d" % g)
+            dst = otile[g][:].rearrange("t (p r) -> t p r", r=rows)[:, :, 4 * s : 4 * s + 4].rearrange(
+                "t p (l h) -> t p l h", l=2
+            )
+            src = obank[j][:].rearrange("t (h l p) -> t p l h", h=2, l=2)
+            nc.scalar.copy(out=dst, in_=src)
+            if s == rows // 4 - 1:
+                finished.append(g)
+
+        def flush_stores():
+            if not late_loaded[0]:
+                return
+            for g in finished[stored[0] :]:
+                nc.sync.dma_start(out=out2[:, bases[g] : bases[g] + P * ROWS[g]], in_=otile[g][:])
+            stored[0] = len(finished)
+
+        last_donor_unit = max([j for j in range(n_units) if units[j][0] == LAST_DONOR])
+
+        finish_stage1()
+        for i in range(n_rounds + 3):
+            for half in range(2):
+                j = 2 * i + half
+                if ok(j):
+                    transposes(j)
+                    regroup(j, 0, "s")
+                    regroup(j, 1, "v")
+                if ok(j - 1):
+                    quantise(j - 1)
+                if ok(j - 5):
+                    copy_out(j - 5)
+            for j in (2 * i - 3, 2 * i - 2):
+                if ok(j):
+                    multiply(j)
+            if last_donor_unit in (2 * i, 2 * i + 1):
+                for g in range(FIRST_LOADS, len(ROWS)):
+                    load_chunk(g)
+                late_loaded[0] = True
+            flush_stores()

@@ -7,6 +7,7 @@ F32 = mybir.dt.float32
 BF16 = mybir.dt.bfloat16
 U32 = mybir.dt.uint32
 U8 = mybir.dt.uint8
+I32 = mybir.dt.int32
 FP8X4 = mybir.dt.float8_e4m3fn_x4
 ADD = mybir.AluOpType.add
 
@@ -15,9 +16,10 @@ T, D, N, DH = 128, 512, 4, 128
 IJ = DH * DH
 FLOPS = 2 * T * D * N * DH + 2 * T * N * DH * IJ
 
-ROWS = [8, 8, 16, 32, 32, 16, 8, 8]
-FIRST_LOADS = 5
-LAST_DONOR = 2
+ROWS = [8, 8, 8, 8, 16, 16, 16, 16, 16, 8, 8]
+FIRST_LOADS = 8
+LAST_DONOR = 4
+EARLY = 4
 MANUAL = True
 
 
@@ -27,9 +29,8 @@ def tile_trittentioncube_pb_kernel(tc, normalized_resid_pre, W_C, b_C, W_K, out)
     with ExitStack() as ctx:
         const = ctx.enter_context(tc.tile_pool(name="const", bufs=1))
         xpools = {
-            8: ctx.enter_context(tc.tile_pool(name="x8", bufs=8)),
-            16: ctx.enter_context(tc.tile_pool(name="x16", bufs=4)),
-            32: ctx.enter_context(tc.tile_pool(name="x32", bufs=8)),
+            8: ctx.enter_context(tc.tile_pool(name="x8", bufs=16)),
+            16: ctx.enter_context(tc.tile_pool(name="x16", bufs=16)),
         }
         opool = ctx.enter_context(tc.tile_pool(name="o", bufs=1))
         gpool = ctx.enter_context(tc.tile_pool(name="g", bufs=3))
@@ -49,8 +50,13 @@ def tile_trittentioncube_pb_kernel(tc, normalized_resid_pre, W_C, b_C, W_K, out)
 
         ident = const.tile([P, P], F32, name="ident")
         make_identity(nc, ident[:])
-        gc = const.tile([P, 4 * T * 4], BF16, name="gc", align_bytes=64)
-        nc.vector.memset(gc[:], 0.0)
+        s_codes = const.tile([P, 4 * T], U32, name="s_codes", align_bytes=64)
+        s_scales = const.tile([P, 4 * T], U8, name="s_scales", align_bytes=64)
+        c_codes = const.tile([P, 2 * T], U32, name="c_codes", align_bytes=64)
+        c_scales = const.tile([P, 2 * T], U8, name="c_scales", align_bytes=64)
+        nc.vector.memset(s_codes[:].bitcast(I32), 0)
+        nc.vector.memset(s_scales[:].bitcast(I32), 0)
+        nc.vector.memset(c_scales[:].bitcast(I32), 0)
 
         x_sb = const.tile([P, D], BF16, name="x_sb")
         nc.sync.dma_start(out=x_sb[:], in_=normalized_resid_pre.rearrange("b t d -> (b t) d"))
@@ -93,64 +99,80 @@ def tile_trittentioncube_pb_kernel(tc, normalized_resid_pre, W_C, b_C, W_K, out)
             out=gx[:].bitcast(F32).rearrange("q (c u) -> q c u", u=2),
             in_=tx[:, 0 : 2 * P].rearrange("q (u c) -> q c u", u=2),
         )
-        bias = [const.tile([P, 4], F32, name="bias%d" % v) for v in range(2)]
-        for v in range(2):
-            nc.vector.tensor_copy(out=bias[v][:], in_=bias_bf[v][:])
         x_codes = const.tile([P, T], U32, name="x_codes", align_bytes=64)
         x_scales = const.tile([P, T], U8, name="x_scales", align_bytes=64)
         nc.vector.quantize_mx(out=x_codes[:].bitcast(FP8X4), scales=x_scales[:], in_=gx[:])
 
-        gw = const.tile([P, 4, 3, 64, 4], BF16, name="gw", align_bytes=64)
+        gw = const.tile([P, 12, 256], BF16, name="gw", align_bytes=64)
         wv = w_raw[:].rearrange("p g f -> p (g f)").rearrange(
             "p (a u t w e) -> p a u t w e", a=2, u=2, t=4, w=64, e=2
         )
-        for u in range(2):
-            for e in range(2):
-                src = wv[:, :, u, :, :, e].rearrange("p a t w -> p a w t")
-                dst = gw[:, 2 * u + e, 0:2, :, :]
-                if u == 0:
-                    nc.vector.tensor_copy(out=dst, in_=src)
-                else:
-                    nc.scalar.copy(out=dst, in_=src)
-        nc.vector.tensor_copy(out=gw[:, :, 2, :, :], in_=gw[:, :, 0, :, :])
+        gws = gw[:].rearrange("p (s z) f -> p s z f", z=3)
+        gwf = gw[:].rearrange("p s f -> p (s f)")
         w_codes = const.tile([P, 768], U32, name="w_codes", align_bytes=64)
         w_scales = const.tile([P, 768], U8, name="w_scales", align_bytes=64)
-        gwf = gw[:].rearrange("p s z w t -> p (s z w t)")
-        nc.vector.quantize_mx(out=w_codes[:, 0:512].bitcast(FP8X4), scales=w_scales[:, 0:512], in_=gwf[:, 0:2048])
-        nc.vector.quantize_mx(
-            out=w_codes[:, 512:768].bitcast(FP8X4), scales=w_scales[:, 512:768], in_=gwf[:, 2048:3072]
-        )
-        pc = []
-        for v in range(2):
-            acc = po.tile([P, 512], F32, name="pc%d" % v, tag="o")
-            for s in range(4):
-                lo = s * 192 + v * 64
-                nc.tensor.matmul_mx(
-                    out=acc[:, s * T : (s + 1) * T],
-                    lhsT=w_codes[:, lo : lo + P].bitcast(FP8X4),
-                    lhsT_scale=w_scales[:, lo : lo + P],
-                    rhs=x_codes[:].bitcast(FP8X4),
-                    rhs_scale=x_scales[:],
-                    start=True,
-                    stop=True,
-                )
-            pc.append(acc)
-        s_codes = const.tile([P, 4 * T], U32, name="s_codes", align_bytes=64)
-        s_scales = const.tile([P, 4 * T], U8, name="s_scales", align_bytes=64)
 
-        def finish_stage1():
+        def regroup_w(u, e, copy):
+            lo = 3 * (2 * u + e)
+            copy(
+                out=gw[:, lo : lo + 2, :].rearrange("p z (w t) -> p z w t", t=4),
+                in_=wv[:, :, u, :, :, e].rearrange("p a t w -> p a w t"),
+            )
+
+        def quantise_w(u):
+            for lo, hi in ((384 * u, 384 * u + 256), (384 * u + 256, 384 * u + 384)):
+                nc.vector.quantize_mx(
+                    out=w_codes[:, lo:hi].bitcast(FP8X4), scales=w_scales[:, lo:hi], in_=gwf[:, 4 * lo : 4 * hi]
+                )
+
+        regroup_w(1, 1, nc.scalar.copy)
+        nc.scalar.copy(
+            out=gw[:, 11, :].rearrange("p (w t) -> p w t", t=4),
+            in_=wv[:, 0, 1, :, :, 1].rearrange("p t w -> p w t"),
+        )
+        regroup_w(0, 0, nc.vector.tensor_copy)
+        regroup_w(0, 1, nc.vector.tensor_copy)
+        nc.vector.tensor_copy(out=gws[:, 0:2, 2, :], in_=gws[:, 0:2, 0, :])
+        regroup_w(1, 0, nc.vector.tensor_copy)
+        quantise_w(0)
+        nc.vector.tensor_copy(out=gws[:, 2, 2, :], in_=gws[:, 2, 0, :])
+        quantise_w(1)
+        bias = [const.tile([P, 4], F32, name="bias%d" % v) for v in range(2)]
+        for v in range(2):
+            nc.vector.tensor_copy(out=bias[v][:], in_=bias_bf[v][:])
+
+        pc = [po.tile([P, 512], F32, name="pc%d" % v, tag="o") for v in range(2)]
+        for u in range(2):
             for v in range(2):
-                for half in range(2):
-                    a = half if v == 0 else 1 - half
-                    slot = 2 * a + half
-                    rows = slice(half * 64, (half + 1) * 64)
-                    nc.vector.tensor_tensor(
-                        out=gc[rows, slot * 512 : (slot + 1) * 512].rearrange("m (c t) -> m c t", t=4),
-                        in0=pc[v][rows, :].rearrange("m (t c) -> m c t", t=4),
-                        in1=bias[v][rows, :].unsqueeze(1).to_broadcast([64, T, 4]),
-                        op=ADD,
+                for e in range(2):
+                    s = 2 * u + e
+                    lo = s * 192 + v * 64
+                    nc.tensor.matmul_mx(
+                        out=pc[v][:, s * T : (s + 1) * T],
+                        lhsT=w_codes[:, lo : lo + P].bitcast(FP8X4),
+                        lhsT_scale=w_scales[:, lo : lo + P],
+                        rhs=x_codes[:].bitcast(FP8X4),
+                        rhs_scale=x_scales[:],
+                        start=True,
+                        stop=True,
                     )
-            nc.vector.quantize_mx(out=s_codes[:].bitcast(FP8X4), scales=s_scales[:], in_=gc[:])
+        cx = const.tile([P, 2 * T * 4], BF16, name="cx", align_bytes=64)
+        for v in range(2):
+            nc.vector.tensor_tensor(
+                out=cx[:, v * 512 : (v + 1) * 512].rearrange("m (c t) -> m c t", t=4),
+                in0=pc[v][:].rearrange("m (t c) -> m c t", t=4),
+                in1=bias[v][:].unsqueeze(1).to_broadcast([P, T, 4]),
+                op=ADD,
+            )
+        nc.vector.quantize_mx(out=c_codes[:].bitcast(FP8X4), scales=c_scales[:], in_=cx[:])
+        for h in range(2):
+            rows = slice(h * 64, (h + 1) * 64)
+            nc.vector.tensor_copy(
+                out=s_codes[rows, h * 256 : (h + 1) * 256].bitcast(I32), in_=c_codes[rows, :].bitcast(I32)
+            )
+            nc.vector.tensor_copy(
+                out=s_scales[rows, h * 256 : (h + 1) * 256].bitcast(I32), in_=c_scales[rows, :].bitcast(I32)
+            )
 
         banks = {}
         grouped = {}
@@ -194,7 +216,7 @@ def tile_trittentioncube_pb_kernel(tc, normalized_resid_pre, W_C, b_C, W_K, out)
             acc = po.tile([P, 512], F32, name="ob%d" % j, tag="o")
             for h in range(2):
                 for a in range(2):
-                    slot = 2 * a + h
+                    slot = 2 * h + (0 if a == h else 1)
                     nc.tensor.matmul_mx(
                         out=acc[:, h * 256 : (h + 1) * 256],
                         lhsT=s_codes[:, slot * T : (slot + 1) * T].bitcast(FP8X4),
@@ -232,14 +254,13 @@ def tile_trittentioncube_pb_kernel(tc, normalized_resid_pre, W_C, b_C, W_K, out)
 
         last_donor_unit = max([j for j in range(n_units) if units[j][0] == LAST_DONOR])
 
-        finish_stage1()
         for i in range(n_rounds + 3):
             for half in range(2):
                 j = 2 * i + half
                 if ok(j):
                     transposes(j)
                     regroup(j, 0, "s")
-                    regroup(j, 1, "v")
+                    regroup(j, 1, "s" if j < EARLY else "v")
                 if ok(j - 1):
                     quantise(j - 1)
                 if ok(j - 5):

@@ -19,6 +19,7 @@ FLOPS = 2 * T * D * N * DH + 2 * T * N * DH * IJ
 ROWS = [8, 8, 8, 8, 16, 16, 16, 16, 16, 8, 8]
 FIRST_LOADS = 8
 LAST_DONOR = 4
+STORES = [[0, 1, 2, 3], [4, 5], [6, 7], [8], [9], [10]]
 EARLY = 4
 MANUAL = True
 
@@ -60,11 +61,10 @@ def tile_trittentioncube_pb_kernel(tc, normalized_resid_pre, W_C, b_C, W_K, out)
 
         x_sb = const.tile([P, D], BF16, name="x_sb")
         nc.sync.dma_start(out=x_sb[:], in_=normalized_resid_pre.rearrange("b t d -> (b t) d"))
-        w_raw = const.tile([P, 8, 256], BF16, name="w_raw")
-        nc.sync.dma_start(
-            out=w_raw[:],
-            in_=W_C.rearrange("n d k -> (n d) k").rearrange("(g p e) k -> p g (e k)", g=8, p=P, e=2),
-        )
+        w_raw = [const.tile([P, 2, 512], BF16, name="w_raw%d" % u) for u in range(2)]
+        wcv = W_C.rearrange("(a u) (p t) k -> u p a (t k)", a=2, u=2, p=P, t=4)
+        for u in range(2):
+            nc.sync.dma_start(out=w_raw[u][:], in_=wcv[u])
         bv = b_C.rearrange("(a u) (w e) -> a w u e", a=2, u=2, w=64, e=2)
         bias_bf = [const.tile([P, 4], BF16, name="bias_bf%d" % v) for v in range(2)]
         for v in range(2):
@@ -93,7 +93,7 @@ def tile_trittentioncube_pb_kernel(tc, normalized_resid_pre, W_C, b_C, W_K, out)
         tx = pt.tile([P, 512], F32, name="tx", tag="t")
         xw = x_sb[:].bitcast(F32)
         for u in range(2):
-            nc.tensor.transpose(tx[:, u * P : (u + 1) * P], xw[:, u * P : (u + 1) * P], ident[:])
+            nc.tensor.transpose(tx[:, u * P : (u + 1) * P], xw[:, u : 2 * P : 2], ident[:])
         gx = const.tile([P, 4 * T], BF16, name="gx", align_bytes=64)
         nc.vector.tensor_copy(
             out=gx[:].bitcast(F32).rearrange("q (c u) -> q c u", u=2),
@@ -104,9 +104,7 @@ def tile_trittentioncube_pb_kernel(tc, normalized_resid_pre, W_C, b_C, W_K, out)
         nc.vector.quantize_mx(out=x_codes[:].bitcast(FP8X4), scales=x_scales[:], in_=gx[:])
 
         gw = const.tile([P, 12, 256], BF16, name="gw", align_bytes=64)
-        wv = w_raw[:].rearrange("p g f -> p (g f)").rearrange(
-            "p (a u t w e) -> p a u t w e", a=2, u=2, t=4, w=64, e=2
-        )
+        wv = [w_raw[u][:].rearrange("p a (t w e) -> p a t w e", t=4, w=64, e=2) for u in range(2)]
         gws = gw[:].rearrange("p (s z) f -> p s z f", z=3)
         gwf = gw[:].rearrange("p s f -> p (s f)")
         w_codes = const.tile([P, 768], U32, name="w_codes", align_bytes=64)
@@ -116,7 +114,7 @@ def tile_trittentioncube_pb_kernel(tc, normalized_resid_pre, W_C, b_C, W_K, out)
             lo = 3 * (2 * u + e)
             copy(
                 out=gw[:, lo : lo + 2, :].rearrange("p z (w t) -> p z w t", t=4),
-                in_=wv[:, :, u, :, :, e].rearrange("p a t w -> p a w t"),
+                in_=wv[u][:, :, :, :, e].rearrange("p a t w -> p a w t"),
             )
 
         def quantise_w(u):
@@ -128,7 +126,7 @@ def tile_trittentioncube_pb_kernel(tc, normalized_resid_pre, W_C, b_C, W_K, out)
         regroup_w(1, 1, nc.scalar.copy)
         nc.scalar.copy(
             out=gw[:, 11, :].rearrange("p (w t) -> p w t", t=4),
-            in_=wv[:, 0, 1, :, :, 1].rearrange("p t w -> p w t"),
+            in_=wv[1][:, 0, :, :, 1].rearrange("p t w -> p w t"),
         )
         regroup_w(0, 0, nc.vector.tensor_copy)
         regroup_w(0, 1, nc.vector.tensor_copy)
@@ -235,21 +233,27 @@ def tile_trittentioncube_pb_kernel(tc, normalized_resid_pre, W_C, b_C, W_K, out)
         def copy_out(j):
             g, s = units[j]
             rows = ROWS[g]
-            if s == 0:
-                otile[g] = opool.tile([P, P * rows], F32, name="o%d" % g)
-            dst = otile[g][:].rearrange("t (p r) -> t p r", r=rows)[:, :, 4 * s : 4 * s + 4].rearrange(
-                "t p (l h) -> t p l h", l=2
+            grp = [q for q in STORES if g in q][0]
+            if s == 0 and g == grp[0]:
+                otile[g] = opool.tile([P, P * sum([ROWS[q] for q in grp])], F32, name="o%d" % g)
+            lo = bases[g] - bases[grp[0]]
+            dst = (
+                otile[grp[0]][:, lo : lo + P * rows]
+                .rearrange("t (p r) -> t p r", r=rows)[:, :, 4 * s : 4 * s + 4]
+                .rearrange("t p (l h) -> t p l h", l=2)
             )
             src = obank[j][:].rearrange("t (h l p) -> t p l h", h=2, l=2)
             nc.scalar.copy(out=dst, in_=src)
-            if s == rows // 4 - 1:
-                finished.append(g)
+            if s == rows // 4 - 1 and g == grp[-1]:
+                finished.append(grp)
 
         def flush_stores():
             if not late_loaded[0]:
                 return
-            for g in finished[stored[0] :]:
-                nc.sync.dma_start(out=out2[:, bases[g] : bases[g] + P * ROWS[g]], in_=otile[g][:])
+            for grp in finished[stored[0] :]:
+                lo = bases[grp[0]]
+                hi = bases[grp[-1]] + P * ROWS[grp[-1]]
+                nc.sync.dma_start(out=out2[:, lo:hi], in_=otile[grp[0]][:])
             stored[0] = len(finished)
 
         last_donor_unit = max([j for j in range(n_units) if units[j][0] == LAST_DONOR])

@@ -20,6 +20,7 @@ ROWS = [8, 8, 8, 8, 16, 16, 16, 16, 16, 8, 8]
 FIRST_LOADS = 8
 LAST_DONOR = 4
 STORES = [[0, 1, 2, 3], [4, 5], [6, 7], [8], [9], [10]]
+ROUNDS = [2, 2, 4, 4, 4, 4, 4, 4, 2, 2]
 EARLY = 4
 MANUAL = True
 
@@ -34,10 +35,10 @@ def tile_trittentioncube_pb_kernel(tc, normalized_resid_pre, W_C, b_C, W_K, out)
             16: ctx.enter_context(tc.tile_pool(name="x16", bufs=16)),
         }
         opool = ctx.enter_context(tc.tile_pool(name="o", bufs=1))
-        gpool = ctx.enter_context(tc.tile_pool(name="g", bufs=3))
-        qpool = ctx.enter_context(tc.tile_pool(name="q", bufs=4))
-        pt = ctx.enter_context(tc.psum_pool(name="pt", bufs=4))
-        po = ctx.enter_context(tc.psum_pool(name="po", bufs=4))
+        gpool = ctx.enter_context(tc.tile_pool(name="g", bufs=5))
+        qpool = ctx.enter_context(tc.tile_pool(name="q", bufs=8))
+        pt = ctx.enter_context(tc.psum_pool(name="pt", bufs=5))
+        po = ctx.enter_context(tc.psum_pool(name="po", bufs=3))
         if MANUAL:
             ctx.enter_context(tc.manual_schedule())
 
@@ -47,7 +48,6 @@ def tile_trittentioncube_pb_kernel(tc, normalized_resid_pre, W_C, b_C, W_K, out)
         bases = [P * sum(ROWS[:g]) for g in range(len(ROWS))]
         units = [(g, s) for g in range(len(ROWS)) for s in range(ROWS[g] // 4)]
         n_units = len(units)
-        n_rounds = n_units // 2
 
         ident = const.tile([P, P], F32, name="ident")
         make_identity(nc, ident[:])
@@ -178,9 +178,6 @@ def tile_trittentioncube_pb_kernel(tc, normalized_resid_pre, W_C, b_C, W_K, out)
         obank = {}
         otile = {}
 
-        def ok(j):
-            return 0 <= j < n_units
-
         def transposes(j):
             g, s = units[j]
             for a in range(2):
@@ -258,21 +255,21 @@ def tile_trittentioncube_pb_kernel(tc, normalized_resid_pre, W_C, b_C, W_K, out)
 
         last_donor_unit = max([j for j in range(n_units) if units[j][0] == LAST_DONOR])
 
-        for i in range(n_rounds + 3):
-            for half in range(2):
-                j = 2 * i + half
-                if ok(j):
-                    transposes(j)
-                    regroup(j, 0, "s")
-                    regroup(j, 1, "s" if j < EARLY else "v")
-                if ok(j - 1):
-                    quantise(j - 1)
-                if ok(j - 5):
-                    copy_out(j - 5)
-            for j in (2 * i - 3, 2 * i - 2):
-                if ok(j):
-                    multiply(j)
-            if last_donor_unit in (2 * i, 2 * i + 1):
+        assert sum(ROUNDS) == n_units
+        first_unit = [sum(ROUNDS[:i]) for i in range(len(ROUNDS) + 1)] + [n_units]
+        for i in range(len(ROUNDS) + 1):
+            now = range(first_unit[i], first_unit[i + 1])
+            before = range(first_unit[i - 1], first_unit[i]) if i > 0 else range(0)
+            for j in now:
+                transposes(j)
+                regroup(j, 0, "s")
+                regroup(j, 1, "s" if j < EARLY else "v")
+            for j in now:
+                quantise(j)
+            for j in before:
+                multiply(j)
+                copy_out(j)
+            if last_donor_unit in now:
                 for g in range(FIRST_LOADS, len(ROWS)):
                     load_chunk(g)
                 late_loaded[0] = True

@@ -16,10 +16,10 @@ T, D, N, DH = 128, 512, 4, 128
 IJ = DH * DH
 FLOPS = 2 * T * D * N * DH + 2 * T * N * DH * IJ
 
-ROWS = [8, 8, 8, 8, 16, 16, 16, 16, 16, 8, 8]
-FIRST_LOADS = 8
-LAST_DONOR = 4
-STORES = [[0, 1, 2, 3], [4, 5], [6, 7], [8], [9], [10]]
+ROWS = [16, 16, 16, 16, 16, 16, 16, 8, 8]
+FIRST_LOADS = 6
+LAST_DONOR = 2
+STORES = [[0, 1], [2, 3], [4, 5], [6], [7], [8]]
 ROUNDS = [2, 2, 4, 4, 4, 4, 4, 4, 2, 2]
 EARLY = 4
 MANUAL = True
@@ -30,10 +30,7 @@ def tile_trittentioncube_pb_kernel(tc, normalized_resid_pre, W_C, b_C, W_K, out)
     assert sum(ROWS) * P == IJ
     with ExitStack() as ctx:
         const = ctx.enter_context(tc.tile_pool(name="const", bufs=1))
-        xpools = {
-            8: ctx.enter_context(tc.tile_pool(name="x8", bufs=16)),
-            16: ctx.enter_context(tc.tile_pool(name="x16", bufs=16)),
-        }
+        xpool = ctx.enter_context(tc.tile_pool(name="x", bufs=4 * FIRST_LOADS))
         opool = ctx.enter_context(tc.tile_pool(name="o", bufs=1))
         gpool = ctx.enter_context(tc.tile_pool(name="g", bufs=5))
         qpool = ctx.enter_context(tc.tile_pool(name="q", bufs=8))
@@ -52,12 +49,9 @@ def tile_trittentioncube_pb_kernel(tc, normalized_resid_pre, W_C, b_C, W_K, out)
         ident = const.tile([P, P], F32, name="ident")
         make_identity(nc, ident[:])
         s_codes = const.tile([P, 4 * T], U32, name="s_codes", align_bytes=64)
-        s_scales = const.tile([P, 4 * T], U8, name="s_scales", align_bytes=64)
         c_codes = const.tile([P, 2 * T], U32, name="c_codes", align_bytes=64)
         c_scales = const.tile([P, 2 * T], U8, name="c_scales", align_bytes=64)
         nc.vector.memset(s_codes[:].bitcast(I32), 0)
-        nc.vector.memset(s_scales[:].bitcast(I32), 0)
-        nc.vector.memset(c_scales[:].bitcast(I32), 0)
 
         x_sb = const.tile([P, D], BF16, name="x_sb")
         nc.sync.dma_start(out=x_sb[:], in_=normalized_resid_pre.rearrange("b t d -> (b t) d"))
@@ -65,22 +59,21 @@ def tile_trittentioncube_pb_kernel(tc, normalized_resid_pre, W_C, b_C, W_K, out)
         wcv = W_C.rearrange("(a u) (p t) k -> u p a (t k)", a=2, u=2, p=P, t=4)
         for u in range(2):
             nc.sync.dma_start(out=w_raw[u][:], in_=wcv[u])
-        bv = b_C.rearrange("(a u) (w e) -> a w u e", a=2, u=2, w=64, e=2)
-        bias_bf = [const.tile([P, 4], BF16, name="bias_bf%d" % v) for v in range(2)]
-        for v in range(2):
-            for a in range(2):
-                half = a if v == 0 else 1 - a
-                nc.scalar.dma_start(
-                    out=bias_bf[v][half * 64 : (half + 1) * 64, :].rearrange("w (u e) -> w u e", u=2),
-                    in_=bv[a],
-                )
+        b_rows = const.tile([P, P], F32, name="b_rows")
+        nc.vector.memset(b_rows[:], 0.0)
+        b_bf = b_rows[:].bitcast(BF16)
+        nc.scalar.dma_start(
+            out=b_bf[0:2, :].rearrange("u (a k) -> u a k", a=2), in_=b_C.rearrange("(a u) k -> u a k", a=2)
+        )
+        for a in range(2):
+            nc.scalar.dma_start(out=b_bf[2:4, (1 - a) * DH : (2 - a) * DH], in_=b_C[2 * a : 2 * a + 2, :])
 
         xt = {}
 
         def load_chunk(g):
             rows = ROWS[g]
             for n in range(N):
-                t = xpools[rows].tile([P, rows * DH], BF16, name="x%d_%d_%d" % (rows, g, n), tag="x%d" % rows)
+                t = xpool.tile([P, rows * DH], BF16, name="x_%d_%d" % (g, n), tag="x")
                 nc.sync.dma_start(
                     out=t[:],
                     in_=wk[n, bases[g] : bases[g] + P * rows, :].rearrange("(p r) k -> p (r k)", r=rows),
@@ -94,6 +87,8 @@ def tile_trittentioncube_pb_kernel(tc, normalized_resid_pre, W_C, b_C, W_K, out)
         xw = x_sb[:].bitcast(F32)
         for u in range(2):
             nc.tensor.transpose(tx[:, u * P : (u + 1) * P], xw[:, u : 2 * P : 2], ident[:])
+        tb = pt.tile([P, 512], F32, name="tb", tag="t")
+        nc.tensor.transpose(tb[:, 0:P], b_rows[:], ident[:])
         gx = const.tile([P, 4 * T], BF16, name="gx", align_bytes=64)
         nc.vector.tensor_copy(
             out=gx[:].bitcast(F32).rearrange("q (c u) -> q c u", u=2),
@@ -135,9 +130,9 @@ def tile_trittentioncube_pb_kernel(tc, normalized_resid_pre, W_C, b_C, W_K, out)
         quantise_w(0)
         nc.vector.tensor_copy(out=gws[:, 2, 2, :], in_=gws[:, 2, 0, :])
         quantise_w(1)
-        bias = [const.tile([P, 4], F32, name="bias%d" % v) for v in range(2)]
-        for v in range(2):
-            nc.vector.tensor_copy(out=bias[v][:], in_=bias_bf[v][:])
+        bias_all = const.tile([P, 8], F32, name="bias_all")
+        nc.vector.tensor_copy(out=bias_all[:], in_=tb[:, 0:4].bitcast(BF16))
+        bias = [bias_all[:, 4 * v : 4 * v + 4] for v in range(2)]
 
         pc = [po.tile([P, 512], F32, name="pc%d" % v, tag="o") for v in range(2)]
         for u in range(2):
@@ -159,7 +154,7 @@ def tile_trittentioncube_pb_kernel(tc, normalized_resid_pre, W_C, b_C, W_K, out)
             nc.vector.tensor_tensor(
                 out=cx[:, v * 512 : (v + 1) * 512].rearrange("m (c t) -> m c t", t=4),
                 in0=pc[v][:].rearrange("m (t c) -> m c t", t=4),
-                in1=bias[v][:].unsqueeze(1).to_broadcast([P, T, 4]),
+                in1=bias[v].unsqueeze(1).to_broadcast([P, T, 4]),
                 op=ADD,
             )
         nc.vector.quantize_mx(out=c_codes[:].bitcast(FP8X4), scales=c_scales[:], in_=cx[:])
@@ -167,9 +162,6 @@ def tile_trittentioncube_pb_kernel(tc, normalized_resid_pre, W_C, b_C, W_K, out)
             rows = slice(h * 64, (h + 1) * 64)
             nc.vector.tensor_copy(
                 out=s_codes[rows, h * 256 : (h + 1) * 256].bitcast(I32), in_=c_codes[rows, :].bitcast(I32)
-            )
-            nc.vector.tensor_copy(
-                out=s_scales[rows, h * 256 : (h + 1) * 256].bitcast(I32), in_=c_scales[rows, :].bitcast(I32)
             )
 
         banks = {}
@@ -211,11 +203,12 @@ def tile_trittentioncube_pb_kernel(tc, normalized_resid_pre, W_C, b_C, W_K, out)
             acc = po.tile([P, 512], F32, name="ob%d" % j, tag="o")
             for h in range(2):
                 for a in range(2):
-                    slot = 2 * h + (0 if a == h else 1)
+                    v = 0 if a == h else 1
+                    slot = 2 * h + v
                     nc.tensor.matmul_mx(
                         out=acc[:, h * 256 : (h + 1) * 256],
                         lhsT=s_codes[:, slot * T : (slot + 1) * T].bitcast(FP8X4),
-                        lhsT_scale=s_scales[:, slot * T : (slot + 1) * T],
+                        lhsT_scale=c_scales[:, v * T : (v + 1) * T],
                         rhs=codes[:, a * 256 : (a + 1) * 256].bitcast(FP8X4),
                         rhs_scale=scales[:, a * 256 : (a + 1) * 256],
                         start=(a == 0),

@@ -16,10 +16,9 @@ T, D, N, DH = 128, 512, 4, 128
 IJ = DH * DH
 FLOPS = 2 * T * D * N * DH + 2 * T * N * DH * IJ
 
-ROWS = [16, 16, 16, 16, 16, 16, 16, 8, 8]
-FIRST_LOADS = 6
-LAST_DONOR = 2
-STORES = [[0, 1], [2, 3], [4, 5], [6], [7], [8]]
+ROWS = [16, 16, 16, 16, 24, 24, 8, 8]
+AHEAD = 4
+STORES = [[0, 1], [2, 3], [4], [5], [6], [7]]
 ROUNDS = [2, 2, 4, 4, 4, 4, 4, 4, 2, 2]
 EARLY = 4
 MANUAL = True
@@ -30,7 +29,7 @@ def tile_trittentioncube_pb_kernel(tc, normalized_resid_pre, W_C, b_C, W_K, out)
     assert sum(ROWS) * P == IJ
     with ExitStack() as ctx:
         const = ctx.enter_context(tc.tile_pool(name="const", bufs=1))
-        xpool = ctx.enter_context(tc.tile_pool(name="x", bufs=4 * FIRST_LOADS))
+        xpool = ctx.enter_context(tc.tile_pool(name="x", bufs=2 * AHEAD))
         opool = ctx.enter_context(tc.tile_pool(name="o", bufs=1))
         gpool = ctx.enter_context(tc.tile_pool(name="g", bufs=5))
         qpool = ctx.enter_context(tc.tile_pool(name="q", bufs=8))
@@ -72,15 +71,17 @@ def tile_trittentioncube_pb_kernel(tc, normalized_resid_pre, W_C, b_C, W_K, out)
 
         def load_chunk(g):
             rows = ROWS[g]
-            for n in range(N):
-                t = xpool.tile([P, rows * DH], BF16, name="x_%d_%d" % (g, n), tag="x")
+            for a in range(2):
+                t = xpool.tile([P, 2, rows * DH], BF16, name="x_%d_%d" % (g, a), tag="x")
                 nc.sync.dma_start(
                     out=t[:],
-                    in_=wk[n, bases[g] : bases[g] + P * rows, :].rearrange("(p r) k -> p (r k)", r=rows),
+                    in_=wk[2 * a : 2 * a + 2, bases[g] : bases[g] + P * rows, :].rearrange(
+                        "n (p r) k -> p n (r k)", r=rows
+                    ),
                 )
-                xt[(g, n)] = t
+                xt[(g, a)] = t
 
-        for g in range(FIRST_LOADS):
+        for g in range(AHEAD):
             load_chunk(g)
 
         tx = pt.tile([P, 512], F32, name="tx", tag="t")
@@ -175,7 +176,7 @@ def tile_trittentioncube_pb_kernel(tc, normalized_resid_pre, W_C, b_C, W_K, out)
             for a in range(2):
                 bank = pt.tile([P, 512], F32, name="tb%d_%d" % (j, a), tag="t")
                 for u in range(2):
-                    xwv = xt[(g, 2 * a + u)][:].bitcast(F32)
+                    xwv = xt[(g, a)][:, u, :].bitcast(F32)
                     for l in range(2):
                         off = (2 * s + l) * P
                         col = (2 * u + l) * P
@@ -218,7 +219,7 @@ def tile_trittentioncube_pb_kernel(tc, normalized_resid_pre, W_C, b_C, W_K, out)
 
         finished = []
         stored = [0]
-        late_loaded = [False]
+        loaded = [AHEAD]
 
         def copy_out(j):
             g, s = units[j]
@@ -238,7 +239,7 @@ def tile_trittentioncube_pb_kernel(tc, normalized_resid_pre, W_C, b_C, W_K, out)
                 finished.append(grp)
 
         def flush_stores():
-            if not late_loaded[0]:
+            if loaded[0] < len(ROWS):
                 return
             for grp in finished[stored[0] :]:
                 lo = bases[grp[0]]
@@ -246,7 +247,7 @@ def tile_trittentioncube_pb_kernel(tc, normalized_resid_pre, W_C, b_C, W_K, out)
                 nc.sync.dma_start(out=out2[:, lo:hi], in_=otile[grp[0]][:])
             stored[0] = len(finished)
 
-        last_donor_unit = max([j for j in range(n_units) if units[j][0] == LAST_DONOR])
+        last_unit = [max([j for j in range(n_units) if units[j][0] == g]) for g in range(len(ROWS))]
 
         assert sum(ROUNDS) == n_units
         first_unit = [sum(ROUNDS[:i]) for i in range(len(ROUNDS) + 1)] + [n_units]
@@ -262,8 +263,7 @@ def tile_trittentioncube_pb_kernel(tc, normalized_resid_pre, W_C, b_C, W_K, out)
             for j in before:
                 multiply(j)
                 copy_out(j)
-            if last_donor_unit in now:
-                for g in range(FIRST_LOADS, len(ROWS)):
-                    load_chunk(g)
-                late_loaded[0] = True
+            while loaded[0] < len(ROWS) and last_unit[loaded[0] - AHEAD] < first_unit[i + 1]:
+                load_chunk(loaded[0])
+                loaded[0] += 1
             flush_stores()

@@ -21,7 +21,7 @@ AHEAD = 4
 STORES = [[0, 1], [2, 3], [4], [5], [6], [7]]
 ROUNDS = [2, 2, 4, 4, 4, 4, 4, 4, 2, 2]
 EARLY = 4
-MANUAL = True
+MANUAL = False
 
 
 def tile_trittentioncube_pb_kernel(tc, normalized_resid_pre, W_C, b_C, W_K, out):

@@ -16,12 +16,12 @@ T, D, N, DH = 128, 512, 4, 128
 IJ = DH * DH
 FLOPS = 2 * T * D * N * DH + 2 * T * N * DH * IJ
 
-ROWS = [16, 16, 16, 16, 24, 24, 8, 8]
+ROWS = [16, 16, 16, 16, 24, 24, 16]
 AHEAD = 4
-STORES = [[0, 1], [2, 3], [4], [5], [6], [7]]
+STORES = [[0, 1], [2, 3], [4], [5], [6]]
 ROUNDS = [2, 2, 4, 4, 4, 4, 4, 4, 2, 2]
 EARLY = 4
-MANUAL = False
+MANUAL = True
 
 
 def tile_trittentioncube_pb_kernel(tc, normalized_resid_pre, W_C, b_C, W_K, out):

@@ -16,12 +16,13 @@ T, D, N, DH = 128, 512, 4, 128
 IJ = DH * DH
 FLOPS = 2 * T * D * N * DH + 2 * T * N * DH * IJ
 
-ROWS = [16, 16, 16, 16, 24, 24, 16]
-AHEAD = 4
-STORES = [[0, 1], [2, 3], [4], [5], [6]]
+ROWS = [8, 16, 16, 16, 16, 16, 16, 16, 8]
+AHEAD = 6
+STORES = [[0, 1], [2, 3], [4], [5], [6], [7], [8]]
 ROUNDS = [2, 2, 4, 4, 4, 4, 4, 4, 2, 2]
 EARLY = 4
 MANUAL = True
+HEAD = 1
 
 
 def tile_trittentioncube_pb_kernel(tc, normalized_resid_pre, W_C, b_C, W_K, out):
@@ -50,7 +51,6 @@ def tile_trittentioncube_pb_kernel(tc, normalized_resid_pre, W_C, b_C, W_K, out)
         s_codes = const.tile([P, 4 * T], U32, name="s_codes", align_bytes=64)
         c_codes = const.tile([P, 2 * T], U32, name="c_codes", align_bytes=64)
         c_scales = const.tile([P, 2 * T], U8, name="c_scales", align_bytes=64)
-        nc.vector.memset(s_codes[:].bitcast(I32), 0)
 
         x_sb = const.tile([P, D], BF16, name="x_sb")
         nc.sync.dma_start(out=x_sb[:], in_=normalized_resid_pre.rearrange("b t d -> (b t) d"))
@@ -60,12 +60,13 @@ def tile_trittentioncube_pb_kernel(tc, normalized_resid_pre, W_C, b_C, W_K, out)
             nc.sync.dma_start(out=w_raw[u][:], in_=wcv[u])
         b_rows = const.tile([P, P], F32, name="b_rows")
         nc.vector.memset(b_rows[:], 0.0)
+        nc.vector.memset(s_codes[:].bitcast(I32), 0)
         b_bf = b_rows[:].bitcast(BF16)
-        nc.scalar.dma_start(
+        nc.sync.dma_start(
             out=b_bf[0:2, :].rearrange("u (a k) -> u a k", a=2), in_=b_C.rearrange("(a u) k -> u a k", a=2)
         )
         for a in range(2):
-            nc.scalar.dma_start(out=b_bf[2:4, (1 - a) * DH : (2 - a) * DH], in_=b_C[2 * a : 2 * a + 2, :])
+            nc.sync.dma_start(out=b_bf[2:4, (1 - a) * DH : (2 - a) * DH], in_=b_C[2 * a : 2 * a + 2, :])
 
         xt = {}
 
@@ -84,12 +85,38 @@ def tile_trittentioncube_pb_kernel(tc, normalized_resid_pre, W_C, b_C, W_K, out)
         for g in range(AHEAD):
             load_chunk(g)
 
+        banks = {}
+        grouped = {}
+        quant = {}
+        obank = {}
+        otile = {}
+
+        def transposes(j):
+            g, s = units[j]
+            for a in range(2):
+                bank = pt.tile([P, 512], F32, name="tb%d_%d" % (j, a), tag="t")
+                for u in range(2):
+                    xwv = xt[(g, a)][:, u, :].bitcast(F32)
+                    for l in range(2):
+                        off = (2 * s + l) * P
+                        col = (2 * u + l) * P
+                        nc.tensor.transpose(bank[:, col : col + P], xwv[:, off : off + P], ident[:])
+                banks[(j, a)] = bank
+
+        def regroup(j, a, eng):
+            if a == 0:
+                grouped[j] = gpool.tile([P, 2048], BF16, name="g%d" % j, tag="g", align_bytes=64)
+            dst = grouped[j][:].bitcast(F32)[:, a * 512 : (a + 1) * 512].rearrange("q (c u) -> q c u", u=2)
+            src = banks[(j, a)][:].rearrange("q (u c) -> q c u", u=2)
+            if eng == "s":
+                nc.scalar.copy(out=dst, in_=src)
+            else:
+                nc.vector.tensor_copy(out=dst, in_=src)
+
         tx = pt.tile([P, 512], F32, name="tx", tag="t")
         xw = x_sb[:].bitcast(F32)
         for u in range(2):
             nc.tensor.transpose(tx[:, u * P : (u + 1) * P], xw[:, u : 2 * P : 2], ident[:])
-        tb = pt.tile([P, 512], F32, name="tb", tag="t")
-        nc.tensor.transpose(tb[:, 0:P], b_rows[:], ident[:])
         gx = const.tile([P, 4 * T], BF16, name="gx", align_bytes=64)
         nc.vector.tensor_copy(
             out=gx[:].bitcast(F32).rearrange("q (c u) -> q c u", u=2),
@@ -131,9 +158,10 @@ def tile_trittentioncube_pb_kernel(tc, normalized_resid_pre, W_C, b_C, W_K, out)
         quantise_w(0)
         nc.vector.tensor_copy(out=gws[:, 2, 2, :], in_=gws[:, 2, 0, :])
         quantise_w(1)
-        bias_all = const.tile([P, 8], F32, name="bias_all")
-        nc.vector.tensor_copy(out=bias_all[:], in_=tb[:, 0:4].bitcast(BF16))
-        bias = [bias_all[:, 4 * v : 4 * v + 4] for v in range(2)]
+        for j in range(HEAD):
+            transposes(j)
+            regroup(j, 0, "s")
+            regroup(j, 1, "s")
 
         pc = [po.tile([P, 512], F32, name="pc%d" % v, tag="o") for v in range(2)]
         for u in range(2):
@@ -150,6 +178,12 @@ def tile_trittentioncube_pb_kernel(tc, normalized_resid_pre, W_C, b_C, W_K, out)
                         start=True,
                         stop=True,
                     )
+        tb = pt.tile([P, 512], F32, name="tb", tag="t")
+        nc.tensor.transpose(tb[:, 0:P], b_rows[:], ident[:])
+        bias_all = const.tile([P, 8], F32, name="bias_all")
+        nc.vector.tensor_copy(out=bias_all[:], in_=tb[:, 0:4].bitcast(BF16))
+        bias = [bias_all[:, 4 * v : 4 * v + 4] for v in range(2)]
+
         cx = const.tile([P, 2 * T * 4], BF16, name="cx", align_bytes=64)
         for v in range(2):
             nc.vector.tensor_tensor(
@@ -164,34 +198,6 @@ def tile_trittentioncube_pb_kernel(tc, normalized_resid_pre, W_C, b_C, W_K, out)
             nc.vector.tensor_copy(
                 out=s_codes[rows, h * 256 : (h + 1) * 256].bitcast(I32), in_=c_codes[rows, :].bitcast(I32)
             )
-
-        banks = {}
-        grouped = {}
-        quant = {}
-        obank = {}
-        otile = {}
-
-        def transposes(j):
-            g, s = units[j]
-            for a in range(2):
-                bank = pt.tile([P, 512], F32, name="tb%d_%d" % (j, a), tag="t")
-                for u in range(2):
-                    xwv = xt[(g, a)][:, u, :].bitcast(F32)
-                    for l in range(2):
-                        off = (2 * s + l) * P
-                        col = (2 * u + l) * P
-                        nc.tensor.transpose(bank[:, col : col + P], xwv[:, off : off + P], ident[:])
-                banks[(j, a)] = bank
-
-        def regroup(j, a, eng):
-            if a == 0:
-                grouped[j] = gpool.tile([P, 2048], BF16, name="g%d" % j, tag="g", align_bytes=64)
-            dst = grouped[j][:].bitcast(F32)[:, a * 512 : (a + 1) * 512].rearrange("q (c u) -> q c u", u=2)
-            src = banks[(j, a)][:].rearrange("q (u c) -> q c u", u=2)
-            if eng == "s":
-                nc.scalar.copy(out=dst, in_=src)
-            else:
-                nc.vector.tensor_copy(out=dst, in_=src)
 
         def quantise(j):
             codes = qpool.tile([P, 512], U32, name="qc%d" % j, tag="qc", align_bytes=64)
@@ -255,6 +261,8 @@ def tile_trittentioncube_pb_kernel(tc, normalized_resid_pre, W_C, b_C, W_K, out)
             now = range(first_unit[i], first_unit[i + 1])
             before = range(first_unit[i - 1], first_unit[i]) if i > 0 else range(0)
             for j in now:
+                if j < HEAD:
+                    continue
                 transposes(j)
                 regroup(j, 0, "s")
                 regroup(j, 1, "s" if j < EARLY else "v")

@@ -16,7 +16,8 @@ T, D, N, DH = 128, 512, 4, 128
 IJ = DH * DH
 FLOPS = 2 * T * D * N * DH + 2 * T * N * DH * IJ
 
-ROWS = [8, 16, 16, 16, 16, 16, 16, 16, 8]
+Q = 32
+ROWS = [32, 64, 64, 64, 64, 64, 64, 64, 32]
 AHEAD = 6
 STORES = [[0, 1], [2, 3], [4], [5], [6], [7], [8]]
 ROUNDS = [2, 2, 4, 4, 4, 4, 4, 4, 2, 2]
@@ -27,10 +28,10 @@ HEAD = 1
 
 def tile_trittentioncube_pb_kernel(tc, normalized_resid_pre, W_C, b_C, W_K, out):
     nc = tc.nc
-    assert sum(ROWS) * P == IJ
+    assert sum(ROWS) * Q == IJ
     with ExitStack() as ctx:
         const = ctx.enter_context(tc.tile_pool(name="const", bufs=1))
-        xpool = ctx.enter_context(tc.tile_pool(name="x", bufs=2 * AHEAD))
+        xpool = ctx.enter_context(tc.tile_pool(name="x", bufs=AHEAD))
         opool = ctx.enter_context(tc.tile_pool(name="o", bufs=1))
         gpool = ctx.enter_context(tc.tile_pool(name="g", bufs=5))
         qpool = ctx.enter_context(tc.tile_pool(name="q", bufs=8))
@@ -42,8 +43,8 @@ def tile_trittentioncube_pb_kernel(tc, normalized_resid_pre, W_C, b_C, W_K, out)
         wk = W_K.rearrange("n i j k -> n (i j) k")
         out2 = out.rearrange("b t i j -> (b t) (i j)")
 
-        bases = [P * sum(ROWS[:g]) for g in range(len(ROWS))]
-        units = [(g, s) for g in range(len(ROWS)) for s in range(ROWS[g] // 4)]
+        bases = [Q * sum(ROWS[:g]) for g in range(len(ROWS))]
+        units = [(g, s) for g in range(len(ROWS)) for s in range(ROWS[g] // 16)]
         n_units = len(units)
 
         ident = const.tile([P, P], F32, name="ident")
@@ -72,15 +73,12 @@ def tile_trittentioncube_pb_kernel(tc, normalized_resid_pre, W_C, b_C, W_K, out)
 
         def load_chunk(g):
             rows = ROWS[g]
-            for a in range(2):
-                t = xpool.tile([P, 2, rows * DH], BF16, name="x_%d_%d" % (g, a), tag="x")
+            xt[g] = xpool.tile([P, rows * DH], BF16, name="x_%d" % g, tag="x")
+            for n in range(N):
                 nc.sync.dma_start(
-                    out=t[:],
-                    in_=wk[2 * a : 2 * a + 2, bases[g] : bases[g] + P * rows, :].rearrange(
-                        "n (p r) k -> p n (r k)", r=rows
-                    ),
+                    out=xt[g][n:P:N, :],
+                    in_=wk[n, bases[g] : bases[g] + Q * rows, :].rearrange("(p r) k -> p (r k)", r=rows),
                 )
-                xt[(g, a)] = t
 
         for g in range(AHEAD):
             load_chunk(g)
@@ -93,21 +91,19 @@ def tile_trittentioncube_pb_kernel(tc, normalized_resid_pre, W_C, b_C, W_K, out)
 
         def transposes(j):
             g, s = units[j]
-            for a in range(2):
-                bank = pt.tile([P, 512], F32, name="tb%d_%d" % (j, a), tag="t")
-                for u in range(2):
-                    xwv = xt[(g, a)][:, u, :].bitcast(F32)
-                    for l in range(2):
-                        off = (2 * s + l) * P
-                        col = (2 * u + l) * P
-                        nc.tensor.transpose(bank[:, col : col + P], xwv[:, off : off + P], ident[:])
-                banks[(j, a)] = bank
+            xw = xt[g][:].bitcast(F32)
+            for b in range(2):
+                bank = pt.tile([P, 512], F32, name="tb%d_%d" % (j, b), tag="t")
+                for i in range(4):
+                    off = (8 * s + 4 * b + i) * P
+                    nc.tensor.transpose(bank[:, i * P : (i + 1) * P], xw[:, off : off + P], ident[:])
+                banks[(j, b)] = bank
 
-        def regroup(j, a, eng):
-            if a == 0:
+        def regroup(j, b, eng):
+            if b == 0:
                 grouped[j] = gpool.tile([P, 2048], BF16, name="g%d" % j, tag="g", align_bytes=64)
-            dst = grouped[j][:].bitcast(F32)[:, a * 512 : (a + 1) * 512].rearrange("q (c u) -> q c u", u=2)
-            src = banks[(j, a)][:].rearrange("q (u c) -> q c u", u=2)
+            dst = grouped[j][:].bitcast(F32).rearrange("q (a b c u) -> q b a c u", a=2, b=2, u=2)[:, b]
+            src = banks[(j, b)][:].rearrange("q (c a u) -> q a c u", a=2, u=2)
             if eng == "s":
                 nc.scalar.copy(out=dst, in_=src)
             else:
@@ -232,16 +228,16 @@ def tile_trittentioncube_pb_kernel(tc, normalized_resid_pre, W_C, b_C, W_K, out)
             rows = ROWS[g]
             grp = [q for q in STORES if g in q][0]
             if s == 0 and g == grp[0]:
-                otile[g] = opool.tile([P, P * sum([ROWS[q] for q in grp])], F32, name="o%d" % g)
+                otile[g] = opool.tile([P, Q * sum([ROWS[q] for q in grp])], F32, name="o%d" % g)
             lo = bases[g] - bases[grp[0]]
             dst = (
-                otile[grp[0]][:, lo : lo + P * rows]
-                .rearrange("t (p r) -> t p r", r=rows)[:, :, 4 * s : 4 * s + 4]
-                .rearrange("t p (l h) -> t p l h", l=2)
+                otile[grp[0]][:, lo : lo + Q * rows]
+                .rearrange("t (p r) -> t p r", r=rows)[:, :, 16 * s : 16 * s + 16]
+                .rearrange("t p (b h) -> t p b h", h=2)
             )
-            src = obank[j][:].rearrange("t (h l p) -> t p l h", h=2, l=2)
+            src = obank[j][:].rearrange("t (h b p) -> t p b h", h=2, p=Q)
             nc.scalar.copy(out=dst, in_=src)
-            if s == rows // 4 - 1 and g == grp[-1]:
+            if s == rows // 16 - 1 and g == grp[-1]:
                 finished.append(grp)
 
         def flush_stores():
@@ -249,7 +245,7 @@ def tile_trittentioncube_pb_kernel(tc, normalized_resid_pre, W_C, b_C, W_K, out)
                 return
             for grp in finished[stored[0] :]:
                 lo = bases[grp[0]]
-                hi = bases[grp[-1]] + P * ROWS[grp[-1]]
+                hi = bases[grp[-1]] + Q * ROWS[grp[-1]]
                 nc.sync.dma_start(out=out2[:, lo:hi], in_=otile[grp[0]][:])
             stored[0] = len(finished)
 

@@ -19,11 +19,10 @@ FLOPS = 2 * T * D * N * DH + 2 * T * N * DH * IJ
 Q = 32
 ROWS = [32, 64, 64, 64, 64, 64, 64, 64, 32]
 AHEAD = 6
-STORES = [[0, 1], [2, 3], [4], [5], [6], [7], [8]]
-ROUNDS = [2, 2, 4, 4, 4, 4, 4, 4, 2, 2]
-EARLY = 4
+STORES = [[0, 1, 2, 3], [4, 5], [6], [7], [8]]
+ROUNDS = [4, 2, 4, 4, 4, 4, 4, 4, 2]
+ALONE = (1, 2)
 MANUAL = True
-HEAD = 1
 
 
 def tile_trittentioncube_pb_kernel(tc, normalized_resid_pre, W_C, b_C, W_K, out):
@@ -52,23 +51,19 @@ def tile_trittentioncube_pb_kernel(tc, normalized_resid_pre, W_C, b_C, W_K, out)
         s_codes = const.tile([P, 4 * T], U32, name="s_codes", align_bytes=64)
         c_codes = const.tile([P, 2 * T], U32, name="c_codes", align_bytes=64)
         c_scales = const.tile([P, 2 * T], U8, name="c_scales", align_bytes=64)
-
+        b_rows = const.tile([P, P], F32, name="b_rows")
+        nc.vector.memset(b_rows[:], 0.0)
+        nc.vector.memset(s_codes[:].bitcast(I32), 0)
+        nc.scalar.dma_start(
+            out=b_rows[0:N, :].bitcast(BF16).rearrange("n (h k) -> n h k", h=2),
+            in_=b_C.unsqueeze(1).to_broadcast([N, 2, DH]),
+        )
         x_sb = const.tile([P, D], BF16, name="x_sb")
         nc.sync.dma_start(out=x_sb[:], in_=normalized_resid_pre.rearrange("b t d -> (b t) d"))
         w_raw = [const.tile([P, 2, 512], BF16, name="w_raw%d" % u) for u in range(2)]
         wcv = W_C.rearrange("(a u) (p t) k -> u p a (t k)", a=2, u=2, p=P, t=4)
         for u in range(2):
             nc.sync.dma_start(out=w_raw[u][:], in_=wcv[u])
-        b_rows = const.tile([P, P], F32, name="b_rows")
-        nc.vector.memset(b_rows[:], 0.0)
-        nc.vector.memset(s_codes[:].bitcast(I32), 0)
-        b_bf = b_rows[:].bitcast(BF16)
-        nc.sync.dma_start(
-            out=b_bf[0:2, :].rearrange("u (a k) -> u a k", a=2), in_=b_C.rearrange("(a u) k -> u a k", a=2)
-        )
-        for a in range(2):
-            nc.sync.dma_start(out=b_bf[2:4, (1 - a) * DH : (2 - a) * DH], in_=b_C[2 * a : 2 * a + 2, :])
-
         xt = {}
 
         def load_chunk(g):
@@ -109,6 +104,12 @@ def tile_trittentioncube_pb_kernel(tc, normalized_resid_pre, W_C, b_C, W_K, out)
             else:
                 nc.vector.tensor_copy(out=dst, in_=src)
 
+        def quantise(j):
+            codes = qpool.tile([P, 512], U32, name="qc%d" % j, tag="qc", align_bytes=64)
+            scales = qpool.tile([P, 512], U8, name="qs%d" % j, tag="qs", align_bytes=64)
+            nc.vector.quantize_mx(out=codes[:].bitcast(FP8X4), scales=scales[:], in_=grouped[j][:])
+            quant[j] = (codes, scales)
+
         tx = pt.tile([P, 512], F32, name="tx", tag="t")
         xw = x_sb[:].bitcast(F32)
         for u in range(2):
@@ -147,17 +148,17 @@ def tile_trittentioncube_pb_kernel(tc, normalized_resid_pre, W_C, b_C, W_K, out)
             out=gw[:, 11, :].rearrange("p (w t) -> p w t", t=4),
             in_=wv[1][:, 0, :, :, 1].rearrange("p t w -> p w t"),
         )
+        regroup_w(1, 0, nc.scalar.copy)
         regroup_w(0, 0, nc.vector.tensor_copy)
         regroup_w(0, 1, nc.vector.tensor_copy)
         nc.vector.tensor_copy(out=gws[:, 0:2, 2, :], in_=gws[:, 0:2, 0, :])
-        regroup_w(1, 0, nc.vector.tensor_copy)
         quantise_w(0)
         nc.vector.tensor_copy(out=gws[:, 2, 2, :], in_=gws[:, 2, 0, :])
         quantise_w(1)
-        for j in range(HEAD):
-            transposes(j)
-            regroup(j, 0, "s")
-            regroup(j, 1, "s")
+        transposes(0)
+        regroup(0, 0, "s")
+        regroup(0, 1, "v")
+        quantise(0)
 
         pc = [po.tile([P, 512], F32, name="pc%d" % v, tag="o") for v in range(2)]
         for u in range(2):
@@ -177,7 +178,10 @@ def tile_trittentioncube_pb_kernel(tc, normalized_resid_pre, W_C, b_C, W_K, out)
         tb = pt.tile([P, 512], F32, name="tb", tag="t")
         nc.tensor.transpose(tb[:, 0:P], b_rows[:], ident[:])
         bias_all = const.tile([P, 8], F32, name="bias_all")
-        nc.vector.tensor_copy(out=bias_all[:], in_=tb[:, 0:4].bitcast(BF16))
+        tbb = tb[:, 0:4].bitcast(BF16)
+        nc.vector.tensor_copy(out=bias_all[0:64, :], in_=tbb[0:64, :])
+        for v in range(2):
+            nc.scalar.copy(out=bias_all[64:P, 4 * v : 4 * v + 4], in_=tbb[64:P, 4 - 4 * v : 8 - 4 * v])
         bias = [bias_all[:, 4 * v : 4 * v + 4] for v in range(2)]
 
         cx = const.tile([P, 2 * T * 4], BF16, name="cx", align_bytes=64)
@@ -194,12 +198,6 @@ def tile_trittentioncube_pb_kernel(tc, normalized_resid_pre, W_C, b_C, W_K, out)
             nc.vector.tensor_copy(
                 out=s_codes[rows, h * 256 : (h + 1) * 256].bitcast(I32), in_=c_codes[rows, :].bitcast(I32)
             )
-
-        def quantise(j):
-            codes = qpool.tile([P, 512], U32, name="qc%d" % j, tag="qc", align_bytes=64)
-            scales = qpool.tile([P, 512], U8, name="qs%d" % j, tag="qs", align_bytes=64)
-            nc.vector.quantize_mx(out=codes[:].bitcast(FP8X4), scales=scales[:], in_=grouped[j][:])
-            quant[j] = (codes, scales)
 
         def multiply(j):
             codes, scales = quant[j]
@@ -257,13 +255,14 @@ def tile_trittentioncube_pb_kernel(tc, normalized_resid_pre, W_C, b_C, W_K, out)
             now = range(first_unit[i], first_unit[i + 1])
             before = range(first_unit[i - 1], first_unit[i]) if i > 0 else range(0)
             for j in now:
-                if j < HEAD:
+                if j == 0:
                     continue
                 transposes(j)
                 regroup(j, 0, "s")
-                regroup(j, 1, "s" if j < EARLY else "v")
+                regroup(j, 1, "s" if j in ALONE else "v")
             for j in now:
-                quantise(j)
+                if j > 0:
+                    quantise(j)
             for j in before:
                 multiply(j)
                 copy_out(j)

@@ -17,11 +17,11 @@ IJ = DH * DH
 FLOPS = 2 * T * D * N * DH + 2 * T * N * DH * IJ
 
 Q = 32
-ROWS = [32, 64, 64, 64, 64, 64, 64, 64, 32]
-AHEAD = 6
+ROWS = [32, 48, 64, 64, 64, 64, 64, 64, 48]
+HOLDER = {6: 1, 7: 2, 8: 3}
 STORES = [[0, 1, 2, 3], [4, 5], [6], [7], [8]]
-ROUNDS = [4, 2, 4, 4, 4, 4, 4, 4, 2]
-ALONE = (1, 2)
+ROUNDS = [3, 2, 4, 4, 4, 4, 4, 4, 3]
+ALONE = (1, 2, 3)
 MANUAL = True
 
 
@@ -30,7 +30,7 @@ def tile_trittentioncube_pb_kernel(tc, normalized_resid_pre, W_C, b_C, W_K, out)
     assert sum(ROWS) * Q == IJ
     with ExitStack() as ctx:
         const = ctx.enter_context(tc.tile_pool(name="const", bufs=1))
-        xpool = ctx.enter_context(tc.tile_pool(name="x", bufs=AHEAD))
+        xpool = ctx.enter_context(tc.tile_pool(name="x", bufs=1))
         opool = ctx.enter_context(tc.tile_pool(name="o", bufs=1))
         gpool = ctx.enter_context(tc.tile_pool(name="g", bufs=5))
         qpool = ctx.enter_context(tc.tile_pool(name="q", bufs=8))
@@ -68,14 +68,14 @@ def tile_trittentioncube_pb_kernel(tc, normalized_resid_pre, W_C, b_C, W_K, out)
 
         def load_chunk(g):
             rows = ROWS[g]
-            xt[g] = xpool.tile([P, rows * DH], BF16, name="x_%d" % g, tag="x")
+            xt[g] = xpool.tile([P, rows * DH], BF16, name="x_%d" % g, tag="x%d" % HOLDER.get(g, g))
             for n in range(N):
                 nc.sync.dma_start(
                     out=xt[g][n:P:N, :],
                     in_=wk[n, bases[g] : bases[g] + Q * rows, :].rearrange("(p r) k -> p (r k)", r=rows),
                 )
 
-        for g in range(AHEAD):
+        for g in range(min(HOLDER)):
             load_chunk(g)
 
         banks = {}
@@ -219,7 +219,7 @@ def tile_trittentioncube_pb_kernel(tc, normalized_resid_pre, W_C, b_C, W_K, out)
 
         finished = []
         stored = [0]
-        loaded = [AHEAD]
+        loaded = [min(HOLDER)]
 
         def copy_out(j):
             g, s = units[j]
@@ -266,7 +266,7 @@ def tile_trittentioncube_pb_kernel(tc, normalized_resid_pre, W_C, b_C, W_K, out)
             for j in before:
                 multiply(j)
                 copy_out(j)
-            while loaded[0] < len(ROWS) and last_unit[loaded[0] - AHEAD] < first_unit[i + 1]:
+            while loaded[0] < len(ROWS) and last_unit[HOLDER[loaded[0]]] < first_unit[i + 1]:
                 load_chunk(loaded[0])
                 loaded[0] += 1
             flush_stores()

from contextlib import ExitStack

import concourse.mybir as mybir
from concourse.masks import make_identity

F32 = mybir.dt.float32
BF16 = mybir.dt.bfloat16
U32 = mybir.dt.uint32
U8 = mybir.dt.uint8
I32 = mybir.dt.int32
FP8X4 = mybir.dt.float8_e4m3fn_x4
ADD = mybir.AluOpType.add

P = 128
T, D, N, DH = 128, 512, 4, 128
IJ = DH * DH
FLOPS = 2 * T * D * N * DH + 2 * T * N * DH * IJ

Q = 32
ROWS = [32, 48, 64, 64, 64, 64, 64, 64, 48]
HOLDER = {6: 1, 7: 2, 8: 3}
STORES = [[0, 1, 2, 3], [4, 5], [6], [7], [8]]
ROUNDS = [3, 2, 4, 4, 4, 4, 4, 4, 3]
ALONE = (1, 2, 3)
MANUAL = True


def tile_trittentioncube_pb_kernel(tc, normalized_resid_pre, W_C, b_C, W_K, out):
    nc = tc.nc
    assert sum(ROWS) * Q == IJ
    with ExitStack() as ctx:
        const = ctx.enter_context(tc.tile_pool(name="const", bufs=1))
        xpool = ctx.enter_context(tc.tile_pool(name="x", bufs=1))
        opool = ctx.enter_context(tc.tile_pool(name="o", bufs=1))
        gpool = ctx.enter_context(tc.tile_pool(name="g", bufs=5))
        qpool = ctx.enter_context(tc.tile_pool(name="q", bufs=8))
        pt = ctx.enter_context(tc.psum_pool(name="pt", bufs=5))
        po = ctx.enter_context(tc.psum_pool(name="po", bufs=3))
        if MANUAL:
            ctx.enter_context(tc.manual_schedule())

        wk = W_K.rearrange("n i j k -> n (i j) k")
        out2 = out.rearrange("b t i j -> (b t) (i j)")

        bases = [Q * sum(ROWS[:g]) for g in range(len(ROWS))]
        units = [(g, s) for g in range(len(ROWS)) for s in range(ROWS[g] // 16)]
        n_units = len(units)

        ident = const.tile([P, P], F32, name="ident")
        make_identity(nc, ident[:])
        s_codes = const.tile([P, 4 * T], U32, name="s_codes", align_bytes=64)
        c_codes = const.tile([P, 2 * T], U32, name="c_codes", align_bytes=64)
        c_scales = const.tile([P, 2 * T], U8, name="c_scales", align_bytes=64)
        b_rows = const.tile([P, P], F32, name="b_rows")
        nc.vector.memset(b_rows[:], 0.0)
        nc.vector.memset(s_codes[:].bitcast(I32), 0)
        nc.scalar.dma_start(
            out=b_rows[0:N, :].bitcast(BF16).rearrange("n (h k) -> n h k", h=2),
            in_=b_C.unsqueeze(1).to_broadcast([N, 2, DH]),
        )
        x_sb = const.tile([P, D], BF16, name="x_sb")
        nc.sync.dma_start(out=x_sb[:], in_=normalized_resid_pre.rearrange("b t d -> (b t) d"))
        w_raw = [const.tile([P, 2, 512], BF16, name="w_raw%d" % u) for u in range(2)]
        wcv = W_C.rearrange("(a u) (p t) k -> u p a (t k)", a=2, u=2, p=P, t=4)
        for u in range(2):
            nc.sync.dma_start(out=w_raw[u][:], in_=wcv[u])
        xt = {}

        def load_chunk(g):
            rows = ROWS[g]
            xt[g] = xpool.tile([P, rows * DH], BF16, name="x_%d" % g, tag="x%d" % HOLDER.get(g, g))
            for n in range(N):
                nc.sync.dma_start(
                    out=xt[g][n:P:N, :],
                    in_=wk[n, bases[g] : bases[g] + Q * rows, :].rearrange("(p r) k -> p (r k)", r=rows),
                )

        for g in range(min(HOLDER)):
            load_chunk(g)

        banks = {}
        grouped = {}
        quant = {}
        obank = {}
        otile = {}

        def transposes(j):
            g, s = units[j]
            xw = xt[g][:].bitcast(F32)
            for b in range(2):
                bank = pt.tile([P, 512], F32, name="tb%d_%d" % (j, b), tag="t")
                for i in range(4):
                    off = (8 * s + 4 * b + i) * P
                    nc.tensor.transpose(bank[:, i * P : (i + 1) * P], xw[:, off : off + P], ident[:])
                banks[(j, b)] = bank

        def regroup(j, b, eng):
            if b == 0:
                grouped[j] = gpool.tile([P, 2048], BF16, name="g%d" % j, tag="g", align_bytes=64)
            dst = grouped[j][:].bitcast(F32).rearrange("q (a b c u) -> q b a c u", a=2, b=2, u=2)[:, b]
            src = banks[(j, b)][:].rearrange("q (c a u) -> q a c u", a=2, u=2)
            if eng == "s":
                nc.scalar.copy(out=dst, in_=src)
            else:
                nc.vector.tensor_copy(out=dst, in_=src)

        def quantise(j):
            codes = qpool.tile([P, 512], U32, name="qc%d" % j, tag="qc", align_bytes=64)
            scales = qpool.tile([P, 512], U8, name="qs%d" % j, tag="qs", align_bytes=64)
            nc.vector.quantize_mx(out=codes[:].bitcast(FP8X4), scales=scales[:], in_=grouped[j][:])
            quant[j] = (codes, scales)

        tx = pt.tile([P, 512], F32, name="tx", tag="t")
        xw = x_sb[:].bitcast(F32)
        for u in range(2):
            nc.tensor.transpose(tx[:, u * P : (u + 1) * P], xw[:, u : 2 * P : 2], ident[:])
        gx = const.tile([P, 4 * T], BF16, name="gx", align_bytes=64)
        nc.vector.tensor_copy(
            out=gx[:].bitcast(F32).rearrange("q (c u) -> q c u", u=2),
            in_=tx[:, 0 : 2 * P].rearrange("q (u c) -> q c u", u=2),
        )
        x_codes = const.tile([P, T], U32, name="x_codes", align_bytes=64)
        x_scales = const.tile([P, T], U8, name="x_scales", align_bytes=64)
        nc.vector.quantize_mx(out=x_codes[:].bitcast(FP8X4), scales=x_scales[:], in_=gx[:])

        gw = const.tile([P, 12, 256], BF16, name="gw", align_bytes=64)
        wv = [w_raw[u][:].rearrange("p a (t w e) -> p a t w e", t=4, w=64, e=2) for u in range(2)]
        gws = gw[:].rearrange("p (s z) f -> p s z f", z=3)
        gwf = gw[:].rearrange("p s f -> p (s f)")
        w_codes = const.tile([P, 768], U32, name="w_codes", align_bytes=64)
        w_scales = const.tile([P, 768], U8, name="w_scales", align_bytes=64)

        def regroup_w(u, e, copy):
            lo = 3 * (2 * u + e)
            copy(
                out=gw[:, lo : lo + 2, :].rearrange("p z (w t) -> p z w t", t=4),
                in_=wv[u][:, :, :, :, e].rearrange("p a t w -> p a w t"),
            )

        def quantise_w(u):
            for lo, hi in ((384 * u, 384 * u + 256), (384 * u + 256, 384 * u + 384)):
                nc.vector.quantize_mx(
                    out=w_codes[:, lo:hi].bitcast(FP8X4), scales=w_scales[:, lo:hi], in_=gwf[:, 4 * lo : 4 * hi]
                )

        regroup_w(1, 1, nc.scalar.copy)
        nc.scalar.copy(
            out=gw[:, 11, :].rearrange("p (w t) -> p w t", t=4),
            in_=wv[1][:, 0, :, :, 1].rearrange("p t w -> p w t"),
        )
        regroup_w(1, 0, nc.scalar.copy)
        regroup_w(0, 0, nc.vector.tensor_copy)
        regroup_w(0, 1, nc.vector.tensor_copy)
        nc.vector.tensor_copy(out=gws[:, 0:2, 2, :], in_=gws[:, 0:2, 0, :])
        quantise_w(0)
        nc.vector.tensor_copy(out=gws[:, 2, 2, :], in_=gws[:, 2, 0, :])
        quantise_w(1)
        transposes(0)
        regroup(0, 0, "s")
        regroup(0, 1, "v")
        quantise(0)

        pc = [po.tile([P, 512], F32, name="pc%d" % v, tag="o") for v in range(2)]
        for u in range(2):
            for v in range(2):
                for e in range(2):
                    s = 2 * u + e
                    lo = s * 192 + v * 64
                    nc.tensor.matmul_mx(
                        out=pc[v][:, s * T : (s + 1) * T],
                        lhsT=w_codes[:, lo : lo + P].bitcast(FP8X4),
                        lhsT_scale=w_scales[:, lo : lo + P],
                        rhs=x_codes[:].bitcast(FP8X4),
                        rhs_scale=x_scales[:],
                        start=True,
                        stop=True,
                    )
        tb = pt.tile([P, 512], F32, name="tb", tag="t")
        nc.tensor.transpose(tb[:, 0:P], b_rows[:], ident[:])
        bias_all = const.tile([P, 8], F32, name="bias_all")
        tbb = tb[:, 0:4].bitcast(BF16)
        nc.vector.tensor_copy(out=bias_all[0:64, :], in_=tbb[0:64, :])
        for v in range(2):
            nc.scalar.copy(out=bias_all[64:P, 4 * v : 4 * v + 4], in_=tbb[64:P, 4 - 4 * v : 8 - 4 * v])
        bias = [bias_all[:, 4 * v : 4 * v + 4] for v in range(2)]

        cx = const.tile([P, 2 * T * 4], BF16, name="cx", align_bytes=64)
        for v in range(2):
            nc.vector.tensor_tensor(
                out=cx[:, v * 512 : (v + 1) * 512].rearrange("m (c t) -> m c t", t=4),
                in0=pc[v][:].rearrange("m (t c) -> m c t", t=4),
                in1=bias[v].unsqueeze(1).to_broadcast([P, T, 4]),
                op=ADD,
            )
        nc.vector.quantize_mx(out=c_codes[:].bitcast(FP8X4), scales=c_scales[:], in_=cx[:])
        for h in range(2):
            rows = slice(h * 64, (h + 1) * 64)
            nc.vector.tensor_copy(
                out=s_codes[rows, h * 256 : (h + 1) * 256].bitcast(I32), in_=c_codes[rows, :].bitcast(I32)
            )

        def multiply(j):
            codes, scales = quant[j]
            acc = po.tile([P, 512], F32, name="ob%d" % j, tag="o")
            for h in range(2):
                for a in range(2):
                    v = 0 if a == h else 1
                    slot = 2 * h + v
                    nc.tensor.matmul_mx(
                        out=acc[:, h * 256 : (h + 1) * 256],
                        lhsT=s_codes[:, slot * T : (slot + 1) * T].bitcast(FP8X4),
                        lhsT_scale=c_scales[:, v * T : (v + 1) * T],
                        rhs=codes[:, a * 256 : (a + 1) * 256].bitcast(FP8X4),
                        rhs_scale=scales[:, a * 256 : (a + 1) * 256],
                        start=(a == 0),
                        stop=(a == 1),
                    )
            obank[j] = acc

        finished = []
        stored = [0]
        loaded = [min(HOLDER)]

        def copy_out(j):
            g, s = units[j]
            rows = ROWS[g]
            grp = [q for q in STORES if g in q][0]
            if s == 0 and g == grp[0]:
                otile[g] = opool.tile([P, Q * sum([ROWS[q] for q in grp])], F32, name="o%d" % g)
            lo = bases[g] - bases[grp[0]]
            dst = (
                otile[grp[0]][:, lo : lo + Q * rows]
                .rearrange("t (p r) -> t p r", r=rows)[:, :, 16 * s : 16 * s + 16]
                .rearrange("t p (b h) -> t p b h", h=2)
            )
            src = obank[j][:].rearrange("t (h b p) -> t p b h", h=2, p=Q)
            nc.scalar.copy(out=dst, in_=src)
            if s == rows // 16 - 1 and g == grp[-1]:
                finished.append(grp)

        def flush_stores():
            if loaded[0] < len(ROWS):
                return
            for grp in finished[stored[0] :]:
                lo = bases[grp[0]]
                hi = bases[grp[-1]] + Q * ROWS[grp[-1]]
                nc.sync.dma_start(out=out2[:, lo:hi], in_=otile[grp[0]][:])
            stored[0] = len(finished)

        last_unit = [max([j for j in range(n_units) if units[j][0] == g]) for g in range(len(ROWS))]

        assert sum(ROUNDS) == n_units
        first_unit = [sum(ROUNDS[:i]) for i in range(len(ROUNDS) + 1)] + [n_units]
        for i in range(len(ROUNDS) + 1):
            now = range(first_unit[i], first_unit[i + 1])
            before = range(first_unit[i - 1], first_unit[i]) if i > 0 else range(0)
            for j in now:
                if j == 0:
                    continue
                transposes(j)
                regroup(j, 0, "s")
                regroup(j, 1, "s" if j in ALONE else "v")
            for j in now:
                if j > 0:
                    quantise(j)
            for j in before:
                multiply(j)
                copy_out(j)
            while loaded[0] < len(ROWS) and last_unit[HOLDER[loaded[0]]] < first_unit[i + 1]:
                load_chunk(loaded[0])
                loaded[0] += 1
            flush_stores()
